import numpy as np
import ml_dtypes


def mxq(x, axis, fmt="e4m3"):
    dtype, down = {"e4m3": (ml_dtypes.float8_e4m3fn, 7), "e5m2": (ml_dtypes.float8_e5m2, 14)}[fmt]
    v = np.moveaxis(np.asarray(x, np.float32).astype(ml_dtypes.bfloat16).astype(np.float64), axis, -1)
    blocks = v.reshape(v.shape[:-1] + (-1, 32))
    amax = np.abs(blocks).max(-1, keepdims=True)
    byte = np.maximum(np.where(amax > 0, np.frexp(amax)[1] - 1 + 127, 0) - down, 1)
    scale = np.exp2(byte - 127.0)
    codes = (blocks / scale).astype(np.float32).astype(dtype).astype(np.float64)
    return np.moveaxis((codes * scale).reshape(v.shape), -1, axis)


WIDE = False


def mx_kscale(k):
    if not WIDE:
        return np.ones(k)
    levels = np.array([10, -10, 5, -5, 0])
    a = np.random.permutation(np.resize(levels, k // 512 * 4)).reshape(k // 512, 4)
    idx = np.arange(k)
    return np.exp2(a[idx // 512, idx % 128 // 32])


BF16 = ml_dtypes.bfloat16


def bf(x):
    return np.asarray(x, np.float32).astype(BF16)


def f64(x):
    return np.asarray(x).astype(np.float64)


B, N, NIN, CTX, H, NOUT = 2, 512, 512, 3, 1024, 2
F = NIN * CTX


def shift_down(y, d):
    return np.pad(y[:, :-d, :], ((0, 0), (d, 0), (0, 0)))


def shift_up(y, d):
    return np.pad(y[:, d:, :], ((0, 0), (0, d), (0, 0)))


def context_linear(xq, w, shifts):
    y = xq @ mxq(w[:, :NIN].T, 0, "e4m3")
    c = 1
    for d in range(1, CTX // 2 + 1):
        for shift in shifts:
            y = y + shift(xq @ mxq(w[:, c * NIN:(c + 1) * NIN].T, 0, "e4m3"), d)
            c += 1
    return y


def setup_inputs():
    s, u = mx_kscale(NIN), mx_kscale(H)
    return {"x_l": bf(np.random.standard_normal((B, N, NIN)) * s),
            "W_l": bf(np.random.standard_normal((H, F)) / np.sqrt(F) / np.tile(s, CTX) * u[:, None]),
            "b_l": bf(np.random.standard_normal(H) * 0.3 * u),
            "W_bil": bf(np.random.standard_normal((NOUT, H, H)) * 0.2 / np.sqrt(H) / u[None, :, None])}


def reference(x_l, W_l, b_l, W_bil):
    xq = mxq(f64(x_l), 2, "e4m3")
    hl = np.maximum(context_linear(xq, f64(W_l), (shift_down, shift_up)) + f64(b_l), 0.0)
    wb = f64(W_bil).transpose(1, 0, 2).reshape(H, NOUT * H)
    t = mxq(hl, 2, "e4m3") @ mxq(wb, 0, "e4m3")
    return t.reshape(B, N, NOUT, H)

@@ -1,0 +1,205 @@
+from contextlib import ExitStack
+
+import concourse.mybir as mybir
+from concourse.masks import make_identity
+
+F32 = mybir.dt.float32
+BF16 = mybir.dt.bfloat16
+U32 = mybir.dt.uint32
+U8 = mybir.dt.uint8
+FP8X4 = mybir.dt.float8_e4m3fn_x4
+RELU = mybir.ActivationFunctionType.Relu
+
+P = 128
+PACK = 4
+K_PASS = P * PACK
+BANK = 512
+
+SEQS, POSITIONS, FEATURES, WINDOW, HIDDEN, MAPS = 2, 512, 512, 3, 1024, 2
+H_PASSES = HIDDEN // K_PASS
+H_TILES = HIDDEN // P
+LANES = POSITIONS // P
+X_BLOCKS = LANES + 2
+X_COLS = X_BLOCKS * P
+WORDS = FEATURES // 2
+ROUNDS = MAPS * HIDDEN // BANK
+TOKEN_TILES = SEQS * LANES
+SHIFTS = (0, -1, 1)
+VECTOR_EVERY = 8
+
+FLOPS = 2 * SEQS * POSITIONS * HIDDEN * (WINDOW * FEATURES + MAPS * HIDDEN)
+
+
+def tile_bilinearpairedlayer_pa_kernel(tc, x_l, W_l, b_l, W_bil, out):
+    nc = tc.nc
+    with ExitStack() as ctx:
+        keep = ctx.enter_context(tc.tile_pool(name="keep", bufs=1))
+        w_stage = ctx.enter_context(tc.tile_pool(name="w_stage", bufs=4))
+        h_stage = ctx.enter_context(tc.tile_pool(name="h_stage", bufs=2))
+        b_stage = ctx.enter_context(tc.tile_pool(name="b_stage", bufs=3))
+        o_stage = ctx.enter_context(tc.tile_pool(name="o_stage", bufs=8))
+        psum = ctx.enter_context(tc.psum_pool(name="psum", bufs=8))
+
+        x_raw = []
+        for b in range(SEQS):
+            x_tile = keep.tile([P, LANES * FEATURES], BF16, name="x_raw%d" % b)
+            nc.sync.dma_start(out=x_tile[:], in_=x_l[b].rearrange("(a s) f -> a (s f)", s=LANES))
+            x_raw.append(x_tile)
+
+        wl_view = W_l.rearrange("(g p tp t2) f -> g tp p (t2 f)", g=H_PASSES, p=P, tp=2, t2=2)
+        wl_raw = {}
+        for g in range(H_PASSES):
+            for tp in range(2):
+                wl_tile = keep.tile([P, 2 * WINDOW * FEATURES], BF16, name="wl_raw%d%d" % (g, tp))
+                nc.sync.dma_start(out=wl_tile[:], in_=wl_view[g, tp])
+                wl_raw[(g, tp)] = wl_tile
+
+        bias_bf = keep.tile([P, H_TILES], BF16, name="bias_bf")
+        nc.sync.dma_start(
+            out=bias_bf[:].rearrange("p (g t) -> p g t", g=H_PASSES),
+            in_=b_l.rearrange("(g p t) -> p g t", g=H_PASSES, p=P, t=PACK),
+        )
+
+        wb_raw = {}
+        for k in range(MAPS):
+            for g in range(H_PASSES):
+                wb_tile = keep.tile([P, PACK, HIDDEN], BF16, name="wb_raw%d%d" % (k, g))
+                nc.sync.dma_start(
+                    out=wb_tile[:],
+                    in_=W_bil[k, g * K_PASS : (g + 1) * K_PASS, :].rearrange("(p t) n -> p t n", t=PACK),
+                )
+                wb_raw[(k, g)] = wb_tile
+
+        ident = keep.tile([P, P], F32, name="ident")
+        make_identity(nc, ident[:])
+        bias = keep.tile([P, H_TILES], F32, name="bias")
+        nc.vector.tensor_copy(out=bias[:], in_=bias_bf[:])
+
+        x_grouped = keep.tile([P, SEQS * X_COLS * PACK], BF16, name="x_grouped", align_bytes=64)
+        x_codes = keep.tile([P, SEQS, X_COLS], U32, name="x_codes", align_bytes=64)
+        x_scales = keep.tile([P, SEQS, X_COLS], U8, name="x_scales", align_bytes=64)
+        wl_codes = keep.tile([P, WINDOW, HIDDEN], U32, name="wl_codes", align_bytes=64)
+        wl_scales = keep.tile([P, WINDOW, HIDDEN], U8, name="wl_scales", align_bytes=64)
+        hl_codes = keep.tile([P, H_PASSES, SEQS * POSITIONS], U32, name="hl_codes", align_bytes=64)
+        hl_scales = keep.tile([P, H_PASSES, SEQS * POSITIONS], U8, name="hl_scales", align_bytes=64)
+        wb_codes = keep.tile([P, ROUNDS, H_PASSES, BANK], U32, name="wb_codes", align_bytes=64)
+        wb_scales = keep.tile([P, ROUNDS, H_PASSES, BANK], U8, name="wb_scales", align_bytes=64)
+
+        def transpose_four(words, first_words):
+            bank = psum.tile([P, BANK], F32, tag="bank", name="bank")
+            for i, first in enumerate(first_words):
+                nc.tensor.transpose(bank[:, i * P : (i + 1) * P], words[:, first : first + P], ident[:])
+            return bank[:].rearrange("p (r u a) -> p r a u", r=2, u=2, a=P)
+
+        x_words = x_grouped[:].bitcast(F32).rearrange(
+            "p (b j a u) -> p b j a u", b=SEQS, j=X_BLOCKS, a=P, u=2
+        )
+        x_values = x_grouped[:].rearrange("p (b j a t) -> p b j a t", b=SEQS, j=X_BLOCKS, a=P, t=PACK)
+        for b in range(SEQS):
+            raw_words = x_raw[b][:].bitcast(F32)
+            for sp in range(LANES // 2):
+                firsts = [(2 * sp + r) * WORDS + u * P for r in range(2) for u in range(2)]
+                turned = transpose_four(raw_words, firsts)
+                nc.vector.tensor_copy(out=x_words[:, b, 1 + 2 * sp : 3 + 2 * sp, :, :], in_=turned)
+            nc.vector.memset(x_values[:, b, 0, 0, :], 0.0)
+            nc.vector.tensor_copy(out=x_values[:, b, 0, 1:P, :], in_=x_values[:, b, LANES, 0 : P - 1, :])
+            nc.vector.memset(x_values[:, b, LANES + 1, P - 1, :], 0.0)
+            nc.vector.tensor_copy(out=x_values[:, b, LANES + 1, 0 : P - 1, :], in_=x_values[:, b, 1, 1:P, :])
+            for first, cols in ((0, 4 * P), (4 * P, 2 * P)):
+                start = (b * X_COLS + first) * PACK
+                nc.vector.quantize_mx(
+                    out=x_codes[:, b, first : first + cols].bitcast(FP8X4),
+                    scales=x_scales[:, b, first : first + cols],
+                    in_=x_grouped[:, start : start + cols * PACK],
+                )
+
+        for g in range(H_PASSES):
+            for tp in range(2):
+                raw_words = wl_raw[(g, tp)][:].bitcast(F32)
+                for c in range(WINDOW):
+                    firsts = [(r * WINDOW + c) * WORDS + u * P for r in range(2) for u in range(2)]
+                    turned = transpose_four(raw_words, firsts)
+                    w_grouped = w_stage.tile([P, 2 * P * PACK], BF16, name="w_grouped", align_bytes=64)
+                    nc.scalar.copy(
+                        out=w_grouped[:].bitcast(F32).rearrange("p (r a u) -> p r a u", r=2, a=P, u=2),
+                        in_=turned,
+                    )
+                    cols = slice((2 * g + tp) * 2 * P, (2 * g + tp + 1) * 2 * P)
+                    nc.vector.quantize_mx(
+                        out=wl_codes[:, c, cols].bitcast(FP8X4),
+                        scales=wl_scales[:, c, cols],
+                        in_=w_grouped[:],
+                    )
+
+        def regroup(grouped, rows):
+            nc.vector.tensor_copy(
+                out=grouped.rearrange("p (c i) t -> p c t i", i=4),
+                in_=rows.rearrange("p t (c i) -> p c t i", i=4),
+            )
+
+        def prepare_w_bil(rnd, g):
+            k, half = divmod(rnd, HIDDEN // BANK)
+            b_grouped = b_stage.tile([P, BANK, PACK], BF16, name="b_grouped", align_bytes=64)
+            regroup(b_grouped[:], wb_raw[(k, g)][:, :, half * BANK : (half + 1) * BANK])
+            nc.vector.quantize_mx(
+                out=wb_codes[:, rnd, g, :].bitcast(FP8X4),
+                scales=wb_scales[:, rnd, g, :],
+                in_=b_grouped[:].rearrange("p n t -> p (n t)"),
+            )
+
+        step = 0
+        for g in range(H_PASSES):
+            for b in range(SEQS):
+                h_rows = h_stage.tile([P, PACK, POSITIONS], BF16, name="h_rows")
+                for t in range(PACK):
+                    h_tile = g * PACK + t
+                    acc = psum.tile([P, BANK], F32, tag="bank", name="acc")
+                    for c in range(WINDOW):
+                        first = (1 + SHIFTS[c]) * P
+                        nc.tensor.matmul_mx(
+                            out=acc[:],
+                            lhsT=wl_codes[:, c, h_tile * P : (h_tile + 1) * P].bitcast(FP8X4),
+                            lhsT_scale=wl_scales[:, c, h_tile * P : (h_tile + 1) * P],
+                            rhs=x_codes[:, b, first : first + POSITIONS].bitcast(FP8X4),
+                            rhs_scale=x_scales[:, b, first : first + POSITIONS],
+                            start=(c == 0),
+                            stop=(c == WINDOW - 1),
+                        )
+                    nc.scalar.activation(
+                        out=h_rows[:, t, :], in_=acc[:], func=RELU, bias=bias[:, h_tile : h_tile + 1], scale=1.0
+                    )
+                prepare_w_bil(step // H_PASSES, step % H_PASSES)
+                step += 1
+                h_grouped = h_stage.tile([P, POSITIONS, PACK], BF16, name="h_grouped", align_bytes=64)
+                regroup(h_grouped[:], h_rows[:])
+                nc.vector.quantize_mx(
+                    out=hl_codes[:, g, b * POSITIONS : (b + 1) * POSITIONS].bitcast(FP8X4),
+                    scales=hl_scales[:, g, b * POSITIONS : (b + 1) * POSITIONS],
+                    in_=h_grouped[:].rearrange("p n t -> p (n t)"),
+                )
+
+        out_view = out.rearrange("b (a s) k n -> b s a k n", s=LANES)
+        for rnd in range(ROUNDS):
+            k, half = divmod(rnd, HIDDEN // BANK)
+            if rnd + 2 < ROUNDS:
+                for g in range(H_PASSES):
+                    prepare_w_bil(rnd + 2, g)
+            for m in range(TOKEN_TILES):
+                b, s = divmod(m, LANES)
+                acc = psum.tile([P, BANK], F32, tag="bank", name="acc")
+                for g in range(H_PASSES):
+                    nc.tensor.matmul_mx(
+                        out=acc[:],
+                        lhsT=hl_codes[:, g, m * P : (m + 1) * P].bitcast(FP8X4),
+                        lhsT_scale=hl_scales[:, g, m * P : (m + 1) * P],
+                        rhs=wb_codes[:, rnd, g, :].bitcast(FP8X4),
+                        rhs_scale=wb_scales[:, rnd, g, :],
+                        start=(g == 0),
+                        stop=(g == H_PASSES - 1),
+                    )
+                result = o_stage.tile([P, BANK], F32, name="result")
+                if m % VECTOR_EVERY == VECTOR_EVERY - 1:
+                    nc.vector.tensor_copy(out=result[:], in_=acc[:])
+                else:
+                    nc.scalar.copy(out=result[:], in_=acc[:])
+                nc.sync.dma_start(out=out_view[b, s][:, k, half * BANK : (half + 1) * BANK], in_=result[:])

@@ -25,40 +25,37 @@ WORDS = FEATURES // 2
 ROUNDS = MAPS * HIDDEN // BANK
 TOKEN_TILES = SEQS * LANES
 SHIFTS = (0, -1, 1)
-VECTOR_EVERY = 8
-
 FLOPS = 2 * SEQS * POSITIONS * HIDDEN * (WINDOW * FEATURES + MAPS * HIDDEN)
 
 
 def tile_bilinearpairedlayer_pa_kernel(tc, x_l, W_l, b_l, W_bil, out):
     nc = tc.nc
     with ExitStack() as ctx:
+        ctx.enter_context(tc.manual_schedule())
         keep = ctx.enter_context(tc.tile_pool(name="keep", bufs=1))
         w_stage = ctx.enter_context(tc.tile_pool(name="w_stage", bufs=4))
-        h_stage = ctx.enter_context(tc.tile_pool(name="h_stage", bufs=2))
+        h_stage = ctx.enter_context(tc.tile_pool(name="h_stage", bufs=3))
         b_stage = ctx.enter_context(tc.tile_pool(name="b_stage", bufs=3))
         o_stage = ctx.enter_context(tc.tile_pool(name="o_stage", bufs=8))
         psum = ctx.enter_context(tc.psum_pool(name="psum", bufs=8))
 
-        x_raw = []
-        for b in range(SEQS):
-            x_tile = keep.tile([P, LANES * FEATURES], BF16, name="x_raw%d" % b)
-            nc.sync.dma_start(out=x_tile[:], in_=x_l[b].rearrange("(a s) f -> a (s f)", s=LANES))
-            x_raw.append(x_tile)
-
         wl_view = W_l.rearrange("(g p tp t2) f -> g tp p (t2 f)", g=H_PASSES, p=P, tp=2, t2=2)
+        x_raw = []
         wl_raw = {}
         for g in range(H_PASSES):
+            x_tile = keep.tile([P, LANES * FEATURES], BF16, name="x_raw%d" % g)
+            nc.sync.dma_start(out=x_tile[:], in_=x_l[g].rearrange("(a s) f -> a (s f)", s=LANES))
+            x_raw.append(x_tile)
             for tp in range(2):
                 wl_tile = keep.tile([P, 2 * WINDOW * FEATURES], BF16, name="wl_raw%d%d" % (g, tp))
                 nc.sync.dma_start(out=wl_tile[:], in_=wl_view[g, tp])
                 wl_raw[(g, tp)] = wl_tile
-
-        bias_bf = keep.tile([P, H_TILES], BF16, name="bias_bf")
-        nc.sync.dma_start(
-            out=bias_bf[:].rearrange("p (g t) -> p g t", g=H_PASSES),
-            in_=b_l.rearrange("(g p t) -> p g t", g=H_PASSES, p=P, t=PACK),
-        )
+            if g == 0:
+                bias_bf = keep.tile([P, H_TILES], BF16, name="bias_bf")
+                nc.sync.dma_start(
+                    out=bias_bf[:].rearrange("p (g t) -> p g t", g=H_PASSES),
+                    in_=b_l.rearrange("(g p t) -> p g t", g=H_PASSES, p=P, t=PACK),
+                )
 
         wb_raw = {}
         for k in range(MAPS):
@@ -72,8 +69,6 @@ def tile_bilinearpairedlayer_pa_kernel(tc, x_l, W_l, b_l, W_bil, out):
 
         ident = keep.tile([P, P], F32, name="ident")
         make_identity(nc, ident[:])
-        bias = keep.tile([P, H_TILES], F32, name="bias")
-        nc.vector.tensor_copy(out=bias[:], in_=bias_bf[:])
 
         x_grouped = keep.tile([P, SEQS * X_COLS * PACK], BF16, name="x_grouped", align_bytes=64)
         x_codes = keep.tile([P, SEQS, X_COLS], U32, name="x_codes", align_bytes=64)
@@ -84,6 +79,7 @@ def tile_bilinearpairedlayer_pa_kernel(tc, x_l, W_l, b_l, W_bil, out):
         hl_scales = keep.tile([P, H_PASSES, SEQS * POSITIONS], U8, name="hl_scales", align_bytes=64)
         wb_codes = keep.tile([P, ROUNDS, H_PASSES, BANK], U32, name="wb_codes", align_bytes=64)
         wb_scales = keep.tile([P, ROUNDS, H_PASSES, BANK], U8, name="wb_scales", align_bytes=64)
+        bias = keep.tile([P, H_TILES], F32, name="bias")
 
         def transpose_four(words, first_words):
             bank = psum.tile([P, BANK], F32, tag="bank", name="bank")
@@ -95,17 +91,18 @@ def tile_bilinearpairedlayer_pa_kernel(tc, x_l, W_l, b_l, W_bil, out):
             "p (b j a u) -> p b j a u", b=SEQS, j=X_BLOCKS, a=P, u=2
         )
         x_values = x_grouped[:].rearrange("p (b j a t) -> p b j a t", b=SEQS, j=X_BLOCKS, a=P, t=PACK)
-        for b in range(SEQS):
+
+        def prepare_x(b):
             raw_words = x_raw[b][:].bitcast(F32)
+            nc.vector.memset(x_values[:, b, 0, 0, :], 0.0)
+            nc.vector.memset(x_values[:, b, LANES + 1, P - 1, :], 0.0)
             for sp in range(LANES // 2):
                 firsts = [(2 * sp + r) * WORDS + u * P for r in range(2) for u in range(2)]
                 turned = transpose_four(raw_words, firsts)
-                nc.vector.tensor_copy(out=x_words[:, b, 1 + 2 * sp : 3 + 2 * sp, :, :], in_=turned)
-            nc.vector.memset(x_values[:, b, 0, 0, :], 0.0)
-            nc.vector.tensor_copy(out=x_values[:, b, 0, 1:P, :], in_=x_values[:, b, LANES, 0 : P - 1, :])
-            nc.vector.memset(x_values[:, b, LANES + 1, P - 1, :], 0.0)
+                nc.scalar.copy(out=x_words[:, b, 1 + 2 * sp : 3 + 2 * sp, :, :], in_=turned)
             nc.vector.tensor_copy(out=x_values[:, b, LANES + 1, 0 : P - 1, :], in_=x_values[:, b, 1, 1:P, :])
-            for first, cols in ((0, 4 * P), (4 * P, 2 * P)):
+            nc.vector.tensor_copy(out=x_values[:, b, 0, 1:P, :], in_=x_values[:, b, LANES, 0 : P - 1, :])
+            for first, cols in ((4 * P, 2 * P), (0, 4 * P)):
                 start = (b * X_COLS + first) * PACK
                 nc.vector.quantize_mx(
                     out=x_codes[:, b, first : first + cols].bitcast(FP8X4),
@@ -113,7 +110,7 @@ def tile_bilinearpairedlayer_pa_kernel(tc, x_l, W_l, b_l, W_bil, out):
                     in_=x_grouped[:, start : start + cols * PACK],
                 )
 
-        for g in range(H_PASSES):
+        def prepare_w_l(g):
             for tp in range(2):
                 raw_words = wl_raw[(g, tp)][:].bitcast(F32)
                 for c in range(WINDOW):
@@ -137,53 +134,72 @@ def tile_bilinearpairedlayer_pa_kernel(tc, x_l, W_l, b_l, W_bil, out):
                 in_=rows.rearrange("p t (c i) -> p c t i", i=4),
             )
 
-        def prepare_w_bil(rnd, g):
+        def regroup_w_bil(rnd, g):
             k, half = divmod(rnd, HIDDEN // BANK)
             b_grouped = b_stage.tile([P, BANK, PACK], BF16, name="b_grouped", align_bytes=64)
             regroup(b_grouped[:], wb_raw[(k, g)][:, :, half * BANK : (half + 1) * BANK])
+            return b_grouped
+
+        def quantise_w_bil(rnd, g, b_grouped):
             nc.vector.quantize_mx(
                 out=wb_codes[:, rnd, g, :].bitcast(FP8X4),
                 scales=wb_scales[:, rnd, g, :],
                 in_=b_grouped[:].rearrange("p n t -> p (n t)"),
             )
 
-        step = 0
-        for g in range(H_PASSES):
-            for b in range(SEQS):
-                h_rows = h_stage.tile([P, PACK, POSITIONS], BF16, name="h_rows")
-                for t in range(PACK):
-                    h_tile = g * PACK + t
-                    acc = psum.tile([P, BANK], F32, tag="bank", name="acc")
-                    for c in range(WINDOW):
-                        first = (1 + SHIFTS[c]) * P
-                        nc.tensor.matmul_mx(
-                            out=acc[:],
-                            lhsT=wl_codes[:, c, h_tile * P : (h_tile + 1) * P].bitcast(FP8X4),
-                            lhsT_scale=wl_scales[:, c, h_tile * P : (h_tile + 1) * P],
-                            rhs=x_codes[:, b, first : first + POSITIONS].bitcast(FP8X4),
-                            rhs_scale=x_scales[:, b, first : first + POSITIONS],
-                            start=(c == 0),
-                            stop=(c == WINDOW - 1),
-                        )
-                    nc.scalar.activation(
-                        out=h_rows[:, t, :], in_=acc[:], func=RELU, bias=bias[:, h_tile : h_tile + 1], scale=1.0
+        def first_matmul(g, b):
+            h_rows = h_stage.tile([P, PACK, POSITIONS], BF16, name="h_rows")
+            for t in range(PACK):
+                h_tile = g * PACK + t
+                acc = psum.tile([P, BANK], F32, tag="bank", name="acc")
+                for c in range(WINDOW):
+                    first = (1 + SHIFTS[c]) * P
+                    nc.tensor.matmul_mx(
+                        out=acc[:],
+                        lhsT=wl_codes[:, c, h_tile * P : (h_tile + 1) * P].bitcast(FP8X4),
+                        lhsT_scale=wl_scales[:, c, h_tile * P : (h_tile + 1) * P],
+                        rhs=x_codes[:, b, first : first + POSITIONS].bitcast(FP8X4),
+                        rhs_scale=x_scales[:, b, first : first + POSITIONS],
+                        start=(c == 0),
+                        stop=(c == WINDOW - 1),
                     )
-                prepare_w_bil(step // H_PASSES, step % H_PASSES)
-                step += 1
-                h_grouped = h_stage.tile([P, POSITIONS, PACK], BF16, name="h_grouped", align_bytes=64)
-                regroup(h_grouped[:], h_rows[:])
-                nc.vector.quantize_mx(
-                    out=hl_codes[:, g, b * POSITIONS : (b + 1) * POSITIONS].bitcast(FP8X4),
-                    scales=hl_scales[:, g, b * POSITIONS : (b + 1) * POSITIONS],
-                    in_=h_grouped[:].rearrange("p n t -> p (n t)"),
+                nc.scalar.activation(
+                    out=h_rows[:, t, :], in_=acc[:], func=RELU, bias=bias[:, h_tile : h_tile + 1], scale=1.0
                 )
+            return h_rows
+
+        def quantise_hidden(g, b, h_rows):
+            step = g * SEQS + b
+            b_grouped = regroup_w_bil(step // H_PASSES, step % H_PASSES)
+            h_grouped = h_stage.tile([P, POSITIONS, PACK], BF16, name="h_grouped", align_bytes=64)
+            regroup(h_grouped[:], h_rows[:])
+            quantise_w_bil(step // H_PASSES, step % H_PASSES, b_grouped)
+            nc.vector.quantize_mx(
+                out=hl_codes[:, g, b * POSITIONS : (b + 1) * POSITIONS].bitcast(FP8X4),
+                scales=hl_scales[:, g, b * POSITIONS : (b + 1) * POSITIONS],
+                in_=h_grouped[:].rearrange("p n t -> p (n t)"),
+            )
+
+        prepare_x(0)
+        prepare_w_l(0)
+        nc.vector.tensor_copy(out=bias[:], in_=bias_bf[:])
+        first_rows = first_matmul(0, 0)
+        prepare_x(1)
+        prepare_w_l(1)
+        quantise_hidden(0, 0, first_rows)
+        for g, b in ((0, 1), (1, 0), (1, 1)):
+            quantise_hidden(g, b, first_matmul(g, b))
 
         out_view = out.rearrange("b (a s) k n -> b s a k n", s=LANES)
         for rnd in range(ROUNDS):
             k, half = divmod(rnd, HIDDEN // BANK)
             if rnd + 2 < ROUNDS:
+                pieces = [regroup_w_bil(rnd + 2, g) for g in range(H_PASSES)]
                 for g in range(H_PASSES):
-                    prepare_w_bil(rnd + 2, g)
+                    quantise_w_bil(rnd + 2, g, pieces[g])
+                vector_every = 8
+            else:
+                vector_every = 2
             for m in range(TOKEN_TILES):
                 b, s = divmod(m, LANES)
                 acc = psum.tile([P, BANK], F32, tag="bank", name="acc")
@@ -198,7 +214,7 @@ def tile_bilinearpairedlayer_pa_kernel(tc, x_l, W_l, b_l, W_bil, out):
                         stop=(g == H_PASSES - 1),
                     )
                 result = o_stage.tile([P, BANK], F32, name="result")
-                if m % VECTOR_EVERY == VECTOR_EVERY - 1:
+                if m % vector_every == vector_every - 1:
                     nc.vector.tensor_copy(out=result[:], in_=acc[:])
                 else:
                     nc.scalar.copy(out=result[:], in_=acc[:])

@@ -25,6 +25,8 @@ WORDS = FEATURES // 2
 ROUNDS = MAPS * HIDDEN // BANK
 TOKEN_TILES = SEQS * LANES
 SHIFTS = (0, -1, 1)
+PIECE_LAG = 1
+
 FLOPS = 2 * SEQS * POSITIONS * HIDDEN * (WINDOW * FEATURES + MAPS * HIDDEN)
 
 
@@ -169,11 +171,13 @@ def tile_bilinearpairedlayer_pa_kernel(tc, x_l, W_l, b_l, W_bil, out):
             return h_rows
 
         def quantise_hidden(g, b, h_rows):
-            step = g * SEQS + b
-            b_grouped = regroup_w_bil(step // H_PASSES, step % H_PASSES)
+            piece = g * SEQS + b - PIECE_LAG
+            if piece >= 0:
+                b_grouped = regroup_w_bil(piece // H_PASSES, piece % H_PASSES)
             h_grouped = h_stage.tile([P, POSITIONS, PACK], BF16, name="h_grouped", align_bytes=64)
             regroup(h_grouped[:], h_rows[:])
-            quantise_w_bil(step // H_PASSES, step % H_PASSES, b_grouped)
+            if piece >= 0:
+                quantise_w_bil(piece // H_PASSES, piece % H_PASSES, b_grouped)
             nc.vector.quantize_mx(
                 out=hl_codes[:, g, b * POSITIONS : (b + 1) * POSITIONS].bitcast(FP8X4),
                 scales=hl_scales[:, g, b * POSITIONS : (b + 1) * POSITIONS],
@@ -183,8 +187,8 @@ def tile_bilinearpairedlayer_pa_kernel(tc, x_l, W_l, b_l, W_bil, out):
         prepare_x(0)
         prepare_w_l(0)
         nc.vector.tensor_copy(out=bias[:], in_=bias_bf[:])
-        first_rows = first_matmul(0, 0)
         prepare_x(1)
+        first_rows = first_matmul(0, 0)
         prepare_w_l(1)
         quantise_hidden(0, 0, first_rows)
         for g, b in ((0, 1), (1, 0), (1, 1)):
@@ -193,29 +197,27 @@ def tile_bilinearpairedlayer_pa_kernel(tc, x_l, W_l, b_l, W_bil, out):
         out_view = out.rearrange("b (a s) k n -> b s a k n", s=LANES)
         for rnd in range(ROUNDS):
             k, half = divmod(rnd, HIDDEN // BANK)
-            if rnd + 2 < ROUNDS:
-                pieces = [regroup_w_bil(rnd + 2, g) for g in range(H_PASSES)]
-                for g in range(H_PASSES):
-                    quantise_w_bil(rnd + 2, g, pieces[g])
-                vector_every = 8
-            else:
-                vector_every = 2
-            for m in range(TOKEN_TILES):
-                b, s = divmod(m, LANES)
-                acc = psum.tile([P, BANK], F32, tag="bank", name="acc")
-                for g in range(H_PASSES):
-                    nc.tensor.matmul_mx(
-                        out=acc[:],
-                        lhsT=hl_codes[:, g, m * P : (m + 1) * P].bitcast(FP8X4),
-                        lhsT_scale=hl_scales[:, g, m * P : (m + 1) * P],
-                        rhs=wb_codes[:, rnd, g, :].bitcast(FP8X4),
-                        rhs_scale=wb_scales[:, rnd, g, :],
-                        start=(g == 0),
-                        stop=(g == H_PASSES - 1),
-                    )
-                result = o_stage.tile([P, BANK], F32, name="result")
-                if m % vector_every == vector_every - 1:
-                    nc.vector.tensor_copy(out=result[:], in_=acc[:])
-                else:
-                    nc.scalar.copy(out=result[:], in_=acc[:])
-                nc.sync.dma_start(out=out_view[b, s][:, k, half * BANK : (half + 1) * BANK], in_=result[:])
+            for b in range(SEQS):
+                piece = H_PASSES * SEQS + rnd * SEQS + b - PIECE_LAG
+                if piece < ROUNDS * H_PASSES:
+                    quantise_w_bil(piece // H_PASSES, piece % H_PASSES, regroup_w_bil(piece // H_PASSES, piece % H_PASSES))
+                for s in range(LANES):
+                    m = b * LANES + s
+                    acc = psum.tile([P, BANK], F32, tag="bank", name="acc")
+                    for g in range(H_PASSES):
+                        nc.tensor.matmul_mx(
+                            out=acc[:],
+                            lhsT=hl_codes[:, g, m * P : (m + 1) * P].bitcast(FP8X4),
+                            lhsT_scale=hl_scales[:, g, m * P : (m + 1) * P],
+                            rhs=wb_codes[:, rnd, g, :].bitcast(FP8X4),
+                            rhs_scale=wb_scales[:, rnd, g, :],
+                            start=(g == 0),
+                            stop=(g == H_PASSES - 1),
+                        )
+                    result = o_stage.tile([P, BANK], F32, name="result")
+                    vector_every = 8 if piece < ROUNDS * H_PASSES else 2
+                    if m % vector_every == vector_every - 1:
+                        nc.vector.tensor_copy(out=result[:], in_=acc[:])
+                    else:
+                        nc.scalar.copy(out=result[:], in_=acc[:])
+                    nc.sync.dma_start(out=out_view[b, s][:, k, half * BANK : (half + 1) * BANK], in_=result[:])

@@ -172,11 +172,11 @@ def tile_bilinearpairedlayer_pa_kernel(tc, x_l, W_l, b_l, W_bil, out):
 
         def quantise_hidden(g, b, h_rows):
             piece = g * SEQS + b - PIECE_LAG
-            if piece >= 0:
+            if piece >= H_PASSES:
                 b_grouped = regroup_w_bil(piece // H_PASSES, piece % H_PASSES)
             h_grouped = h_stage.tile([P, POSITIONS, PACK], BF16, name="h_grouped", align_bytes=64)
             regroup(h_grouped[:], h_rows[:])
-            if piece >= 0:
+            if piece >= H_PASSES:
                 quantise_w_bil(piece // H_PASSES, piece % H_PASSES, b_grouped)
             nc.vector.quantize_mx(
                 out=hl_codes[:, g, b * POSITIONS : (b + 1) * POSITIONS].bitcast(FP8X4),
@@ -188,9 +188,11 @@ def tile_bilinearpairedlayer_pa_kernel(tc, x_l, W_l, b_l, W_bil, out):
         prepare_w_l(0)
         nc.vector.tensor_copy(out=bias[:], in_=bias_bf[:])
         prepare_x(1)
-        first_rows = first_matmul(0, 0)
+        quantise_hidden(0, 0, first_matmul(0, 0))
         prepare_w_l(1)
-        quantise_hidden(0, 0, first_rows)
+        round_0 = [regroup_w_bil(0, g) for g in range(H_PASSES)]
+        for g in range(H_PASSES):
+            quantise_w_bil(0, g, round_0[g])
         for g, b in ((0, 1), (1, 0), (1, 1)):
             quantise_hidden(g, b, first_matmul(g, b))
 
@@ -215,8 +217,7 @@ def tile_bilinearpairedlayer_pa_kernel(tc, x_l, W_l, b_l, W_bil, out):
                             stop=(g == H_PASSES - 1),
                         )
                     result = o_stage.tile([P, BANK], F32, name="result")
-                    vector_every = 8 if piece < ROUNDS * H_PASSES else 2
-                    if m % vector_every == vector_every - 1:
+                    if piece >= ROUNDS * H_PASSES and s % 2 == 1:
                         nc.vector.tensor_copy(out=result[:], in_=acc[:])
                     else:
                         nc.scalar.copy(out=result[:], in_=acc[:])

from contextlib import ExitStack

import concourse.mybir as mybir
from concourse.masks import make_identity

F32 = mybir.dt.float32
BF16 = mybir.dt.bfloat16
U32 = mybir.dt.uint32
U8 = mybir.dt.uint8
FP8X4 = mybir.dt.float8_e4m3fn_x4
RELU = mybir.ActivationFunctionType.Relu

P = 128
PACK = 4
K_PASS = P * PACK
BANK = 512

SEQS, POSITIONS, FEATURES, WINDOW, HIDDEN, MAPS = 2, 512, 512, 3, 1024, 2
H_PASSES = HIDDEN // K_PASS
H_TILES = HIDDEN // P
LANES = POSITIONS // P
X_BLOCKS = LANES + 2
X_COLS = X_BLOCKS * P
WORDS = FEATURES // 2
ROUNDS = MAPS * HIDDEN // BANK
TOKEN_TILES = SEQS * LANES
SHIFTS = (0, -1, 1)
PIECE_LAG = 1

FLOPS = 2 * SEQS * POSITIONS * HIDDEN * (WINDOW * FEATURES + MAPS * HIDDEN)


def tile_bilinearpairedlayer_pa_kernel(tc, x_l, W_l, b_l, W_bil, out):
    nc = tc.nc
    with ExitStack() as ctx:
        ctx.enter_context(tc.manual_schedule())
        keep = ctx.enter_context(tc.tile_pool(name="keep", bufs=1))
        w_stage = ctx.enter_context(tc.tile_pool(name="w_stage", bufs=4))
        h_stage = ctx.enter_context(tc.tile_pool(name="h_stage", bufs=3))
        b_stage = ctx.enter_context(tc.tile_pool(name="b_stage", bufs=3))
        o_stage = ctx.enter_context(tc.tile_pool(name="o_stage", bufs=8))
        psum = ctx.enter_context(tc.psum_pool(name="psum", bufs=8))

        wl_view = W_l.rearrange("(g p tp t2) f -> g tp p (t2 f)", g=H_PASSES, p=P, tp=2, t2=2)
        x_raw = []
        wl_raw = {}
        for g in range(H_PASSES):
            x_tile = keep.tile([P, LANES * FEATURES], BF16, name="x_raw%d" % g)
            nc.sync.dma_start(out=x_tile[:], in_=x_l[g].rearrange("(a s) f -> a (s f)", s=LANES))
            x_raw.append(x_tile)
            for tp in range(2):
                wl_tile = keep.tile([P, 2 * WINDOW * FEATURES], BF16, name="wl_raw%d%d" % (g, tp))
                nc.sync.dma_start(out=wl_tile[:], in_=wl_view[g, tp])
                wl_raw[(g, tp)] = wl_tile
            if g == 0:
                bias_bf = keep.tile([P, H_TILES], BF16, name="bias_bf")
                nc.sync.dma_start(
                    out=bias_bf[:].rearrange("p (g t) -> p g t", g=H_PASSES),
                    in_=b_l.rearrange("(g p t) -> p g t", g=H_PASSES, p=P, t=PACK),
                )

        wb_raw = {}
        for k in range(MAPS):
            for g in range(H_PASSES):
                wb_tile = keep.tile([P, PACK, HIDDEN], BF16, name="wb_raw%d%d" % (k, g))
                nc.sync.dma_start(
                    out=wb_tile[:],
                    in_=W_bil[k, g * K_PASS : (g + 1) * K_PASS, :].rearrange("(p t) n -> p t n", t=PACK),
                )
                wb_raw[(k, g)] = wb_tile

        ident = keep.tile([P, P], F32, name="ident")
        make_identity(nc, ident[:])

        x_grouped = keep.tile([P, SEQS * X_COLS * PACK], BF16, name="x_grouped", align_bytes=64)
        x_codes = keep.tile([P, SEQS, X_COLS], U32, name="x_codes", align_bytes=64)
        x_scales = keep.tile([P, SEQS, X_COLS], U8, name="x_scales", align_bytes=64)
        wl_codes = keep.tile([P, WINDOW, HIDDEN], U32, name="wl_codes", align_bytes=64)
        wl_scales = keep.tile([P, WINDOW, HIDDEN], U8, name="wl_scales", align_bytes=64)
        hl_codes = keep.tile([P, H_PASSES, SEQS * POSITIONS], U32, name="hl_codes", align_bytes=64)
        hl_scales = keep.tile([P, H_PASSES, SEQS * POSITIONS], U8, name="hl_scales", align_bytes=64)
        wb_codes = keep.tile([P, ROUNDS, H_PASSES, BANK], U32, name="wb_codes", align_bytes=64)
        wb_scales = keep.tile([P, ROUNDS, H_PASSES, BANK], U8, name="wb_scales", align_bytes=64)
        bias = keep.tile([P, H_TILES], F32, name="bias")

        def transpose_four(words, first_words):
            bank = psum.tile([P, BANK], F32, tag="bank", name="bank")
            for i, first in enumerate(first_words):
                nc.tensor.transpose(bank[:, i * P : (i + 1) * P], words[:, first : first + P], ident[:])
            return bank[:].rearrange("p (r u a) -> p r a u", r=2, u=2, a=P)

        x_words = x_grouped[:].bitcast(F32).rearrange(
            "p (b j a u) -> p b j a u", b=SEQS, j=X_BLOCKS, a=P, u=2
        )
        x_values = x_grouped[:].rearrange("p (b j a t) -> p b j a t", b=SEQS, j=X_BLOCKS, a=P, t=PACK)

        def prepare_x(b):
            raw_words = x_raw[b][:].bitcast(F32)
            nc.vector.memset(x_values[:, b, 0, 0, :], 0.0)
            nc.vector.memset(x_values[:, b, LANES + 1, P - 1, :], 0.0)
            for sp in range(LANES // 2):
                firsts = [(2 * sp + r) * WORDS + u * P for r in range(2) for u in range(2)]
                turned = transpose_four(raw_words, firsts)
                nc.scalar.copy(out=x_words[:, b, 1 + 2 * sp : 3 + 2 * sp, :, :], in_=turned)
            nc.vector.tensor_copy(out=x_values[:, b, LANES + 1, 0 : P - 1, :], in_=x_values[:, b, 1, 1:P, :])
            nc.vector.tensor_copy(out=x_values[:, b, 0, 1:P, :], in_=x_values[:, b, LANES, 0 : P - 1, :])
            for first, cols in ((4 * P, 2 * P), (0, 4 * P)):
                start = (b * X_COLS + first) * PACK
                nc.vector.quantize_mx(
                    out=x_codes[:, b, first : first + cols].bitcast(FP8X4),
                    scales=x_scales[:, b, first : first + cols],
                    in_=x_grouped[:, start : start + cols * PACK],
                )

        def prepare_w_l(g):
            for tp in range(2):
                raw_words = wl_raw[(g, tp)][:].bitcast(F32)
                for c in range(WINDOW):
                    firsts = [(r * WINDOW + c) * WORDS + u * P for r in range(2) for u in range(2)]
                    turned = transpose_four(raw_words, firsts)
                    w_grouped = w_stage.tile([P, 2 * P * PACK], BF16, name="w_grouped", align_bytes=64)
                    nc.scalar.copy(
                        out=w_grouped[:].bitcast(F32).rearrange("p (r a u) -> p r a u", r=2, a=P, u=2),
                        in_=turned,
                    )
                    cols = slice((2 * g + tp) * 2 * P, (2 * g + tp + 1) * 2 * P)
                    nc.vector.quantize_mx(
                        out=wl_codes[:, c, cols].bitcast(FP8X4),
                        scales=wl_scales[:, c, cols],
                        in_=w_grouped[:],
                    )

        def regroup(grouped, rows):
            nc.vector.tensor_copy(
                out=grouped.rearrange("p (c i) t -> p c t i", i=4),
                in_=rows.rearrange("p t (c i) -> p c t i", i=4),
            )

        def regroup_w_bil(rnd, g):
            k, half = divmod(rnd, HIDDEN // BANK)
            b_grouped = b_stage.tile([P, BANK, PACK], BF16, name="b_grouped", align_bytes=64)
            regroup(b_grouped[:], wb_raw[(k, g)][:, :, half * BANK : (half + 1) * BANK])
            return b_grouped

        def quantise_w_bil(rnd, g, b_grouped):
            nc.vector.quantize_mx(
                out=wb_codes[:, rnd, g, :].bitcast(FP8X4),
                scales=wb_scales[:, rnd, g, :],
                in_=b_grouped[:].rearrange("p n t -> p (n t)"),
            )

        def first_matmul(g, b):
            h_rows = h_stage.tile([P, PACK, POSITIONS], BF16, name="h_rows")
            for t in range(PACK):
                h_tile = g * PACK + t
                acc = psum.tile([P, BANK], F32, tag="bank", name="acc")
                for c in range(WINDOW):
                    first = (1 + SHIFTS[c]) * P
                    nc.tensor.matmul_mx(
                        out=acc[:],
                        lhsT=wl_codes[:, c, h_tile * P : (h_tile + 1) * P].bitcast(FP8X4),
                        lhsT_scale=wl_scales[:, c, h_tile * P : (h_tile + 1) * P],
                        rhs=x_codes[:, b, first : first + POSITIONS].bitcast(FP8X4),
                        rhs_scale=x_scales[:, b, first : first + POSITIONS],
                        start=(c == 0),
                        stop=(c == WINDOW - 1),
                    )
                nc.scalar.activation(
                    out=h_rows[:, t, :], in_=acc[:], func=RELU, bias=bias[:, h_tile : h_tile + 1], scale=1.0
                )
            return h_rows

        def quantise_hidden(g, b, h_rows):
            piece = g * SEQS + b - PIECE_LAG
            if piece >= H_PASSES:
                b_grouped = regroup_w_bil(piece // H_PASSES, piece % H_PASSES)
            h_grouped = h_stage.tile([P, POSITIONS, PACK], BF16, name="h_grouped", align_bytes=64)
            regroup(h_grouped[:], h_rows[:])
            if piece >= H_PASSES:
                quantise_w_bil(piece // H_PASSES, piece % H_PASSES, b_grouped)
            nc.vector.quantize_mx(
                out=hl_codes[:, g, b * POSITIONS : (b + 1) * POSITIONS].bitcast(FP8X4),
                scales=hl_scales[:, g, b * POSITIONS : (b + 1) * POSITIONS],
                in_=h_grouped[:].rearrange("p n t -> p (n t)"),
            )

        prepare_x(0)
        prepare_w_l(0)
        nc.vector.tensor_copy(out=bias[:], in_=bias_bf[:])
        prepare_x(1)
        quantise_hidden(0, 0, first_matmul(0, 0))
        prepare_w_l(1)
        round_0 = [regroup_w_bil(0, g) for g in range(H_PASSES)]
        for g in range(H_PASSES):
            quantise_w_bil(0, g, round_0[g])
        for g, b in ((0, 1), (1, 0), (1, 1)):
            quantise_hidden(g, b, first_matmul(g, b))

        out_view = out.rearrange("b (a s) k n -> b s a k n", s=LANES)
        for rnd in range(ROUNDS):
            k, half = divmod(rnd, HIDDEN // BANK)
            for b in range(SEQS):
                piece = H_PASSES * SEQS + rnd * SEQS + b - PIECE_LAG
                if piece < ROUNDS * H_PASSES:
                    quantise_w_bil(piece // H_PASSES, piece % H_PASSES, regroup_w_bil(piece // H_PASSES, piece % H_PASSES))
                for s in range(LANES):
                    m = b * LANES + s
                    acc = psum.tile([P, BANK], F32, tag="bank", name="acc")
                    for g in range(H_PASSES):
                        nc.tensor.matmul_mx(
                            out=acc[:],
                            lhsT=hl_codes[:, g, m * P : (m + 1) * P].bitcast(FP8X4),
                            lhsT_scale=hl_scales[:, g, m * P : (m + 1) * P],
                            rhs=wb_codes[:, rnd, g, :].bitcast(FP8X4),
                            rhs_scale=wb_scales[:, rnd, g, :],
                            start=(g == 0),
                            stop=(g == H_PASSES - 1),
                        )
                    result = o_stage.tile([P, BANK], F32, name="result")
                    if piece >= ROUNDS * H_PASSES and s % 2 == 1:
                        nc.vector.tensor_copy(out=result[:], in_=acc[:])
                    else:
                        nc.scalar.copy(out=result[:], in_=acc[:])
                    nc.sync.dma_start(out=out_view[b, s][:, k, half * BANK : (half + 1) * BANK], in_=result[:])
